import numpy as np
import ml_dtypes


def mxq(x, axis, fmt="e4m3"):
    dtype, down = {"e4m3": (ml_dtypes.float8_e4m3fn, 7), "e5m2": (ml_dtypes.float8_e5m2, 14)}[fmt]
    v = np.moveaxis(np.asarray(x, np.float32).astype(ml_dtypes.bfloat16).astype(np.float64), axis, -1)
    blocks = v.reshape(v.shape[:-1] + (-1, 32))
    amax = np.abs(blocks).max(-1, keepdims=True)
    byte = np.maximum(np.where(amax > 0, np.frexp(amax)[1] - 1 + 127, 0) - down, 1)
    scale = np.exp2(byte - 127.0)
    codes = (blocks / scale).astype(np.float32).astype(dtype).astype(np.float64)
    return np.moveaxis((codes * scale).reshape(v.shape), -1, axis)


WIDE = False


def mx_kscale(k):
    if not WIDE:
        return np.ones(k)
    levels = np.array([10, -10, 5, -5, 0])
    a = np.random.permutation(np.resize(levels, k // 512 * 4)).reshape(k // 512, 4)
    idx = np.arange(k)
    return np.exp2(a[idx // 512, idx % 128 // 32])


BF16 = ml_dtypes.bfloat16


def bf(x):
    return np.asarray(x, np.float32).astype(BF16)


def f64(x):
    return np.asarray(x).astype(np.float64)


B, S, D, QR, KR, H, NOPE, ROPE, VD = 2, 2048, 1024, 1536, 512, 2, 128, 64, 128
EPS = 1e-6
THETA = 10000.0
LAT = 3.0 * np.sqrt(EPS)


def rmsnorm(x, w):
    var = np.mean(x * x, axis=-1, keepdims=True)
    return w * (x * (1.0 / np.sqrt(var + EPS)))


def rope_cos_sin(seq_len):
    inv_freq = 1.0 / (THETA ** (f64(np.arange(0, ROPE, 2)) / ROPE))
    t = f64(np.arange(seq_len))
    freqs = np.outer(t, inv_freq)
    emb = np.concatenate([freqs, freqs], -1)
    return np.cos(emb), np.sin(emb)


def rotate_half(x):
    x1, x2 = x[..., : x.shape[-1] // 2], x[..., x.shape[-1] // 2 :]
    return np.concatenate([-x2, x1], axis=-1)


def setup_inputs():
    s, t = mx_kscale(D), mx_kscale(KR)
    return {"hidden_states": bf(np.random.standard_normal((B, S, D)) * s),
            "kv_a_w_ckv": bf(np.random.standard_normal((KR, D)) * LAT / np.sqrt(D) / s[None, :]),
            "k_pe_raw": bf(np.random.standard_normal((B, S, ROPE))),
            "kv_a_ln_w": bf((1.0 + 0.1 * np.random.standard_normal(KR)) * t),
            "kv_b_w": bf(np.random.standard_normal((H * (NOPE + VD), KR)) / np.sqrt(KR) / t[None, :])}


def reference(hidden_states, kv_a_w_ckv, k_pe_raw, kv_a_ln_w, kv_b_w):
    ckv = mxq(f64(hidden_states), 2, "e4m3") @ mxq(f64(kv_a_w_ckv), 1, "e4m3").T
    ckv_n = rmsnorm(ckv, f64(kv_a_ln_w))
    kv = mxq(ckv_n, 2, "e4m3") @ mxq(f64(kv_b_w), 1, "e4m3").T
    kv = kv.reshape(B, S, H, NOPE + VD).transpose(0, 2, 1, 3)
    k_nope, v = kv[..., :NOPE], kv[..., NOPE:]
    k_pe = f64(k_pe_raw).reshape(B, 1, S, ROPE)
    cos, sin = rope_cos_sin(S)
    cos, sin = cos[None, None], sin[None, None]
    k_pe = k_pe * cos + rotate_half(k_pe) * sin
    key_s = np.concatenate([k_nope, np.broadcast_to(k_pe, (B, H, S, ROPE))], -1)
    return key_s, v

@@ -1,0 +1,276 @@
+from contextlib import ExitStack
+import math
+
+import concourse.bass as bass
+import concourse.mybir as mybir
+import concourse.tile as tile
+from concourse.masks import make_identity
+
+FLOPS = 2 * 4096 * 1024 * 512 + 2 * 4096 * 512 * 512
+
+F32 = mybir.dt.float32
+BF16 = mybir.dt.bfloat16
+I32 = mybir.dt.int32
+U32 = mybir.dt.uint32
+U8 = mybir.dt.uint8
+FP8X4 = mybir.dt.float8_e4m3fn_x4
+ALU = mybir.AluOpType
+ACT = mybir.ActivationFunctionType
+
+P = 128
+EPS = 1e-6
+THETA = 10000.0
+N_PAIRS = 16
+
+
+def tile_modelnew_pb_t_kernel(tc, hidden_states, kv_a_w_ckv, k_pe_raw, kv_a_ln_w, kv_b_w, out_0, out_1):
+    nc = tc.nc
+    with ExitStack() as ctx:
+        const = ctx.enter_context(tc.tile_pool(name="const", bufs=1))
+        work = ctx.enter_context(tc.tile_pool(name="work", bufs=3))
+        outp = ctx.enter_context(tc.tile_pool(name="outp", bufs=4))
+        xtp = ctx.enter_context(tc.psum_pool(name="xtp", bufs=2))
+        ckp = ctx.enter_context(tc.psum_pool(name="ckp", bufs=3))
+        t2p = ctx.enter_context(tc.psum_pool(name="t2p", bufs=1))
+        kvp = ctx.enter_context(tc.psum_pool(name="kvp", bufs=2))
+        ctx.enter_context(tc.manual_schedule())
+
+        hs_v = hidden_states.flatten_outer_dims().rearrange("(c p j) d -> c p (j d)", p=P, j=4)
+        wa_sb = const.tile([P, 4, 1024], BF16, name="wa_sb")
+        nc.sync.dma_start(out=wa_sb[:].rearrange("p a d -> p (a d)"), in_=kv_a_w_ckv.rearrange("(p a) d -> p (a d)", a=4))
+        hs_sb = []
+        for c in range(8):
+            hs_c = const.tile([P, 4, 1024], BF16, name="hs%d" % c)
+            hs_sb.append(hs_c)
+        nc.sync.dma_start(out=hs_sb[0][:].rearrange("p j d -> p (j d)"), in_=hs_v[0])
+        wb_sb = const.tile([P, 4, 512], BF16, name="wb_sb")
+        nc.sync.dma_start(out=wb_sb[:], in_=kv_b_w.rearrange("(a p) k -> p a k", p=P))
+        for c in range(1, 8):
+            nc.sync.dma_start(out=hs_sb[c][:].rearrange("p j d -> p (j d)"), in_=hs_v[c])
+        kpe = const.tile([P, 8, 256], BF16, name="kpe")
+        nc.scalar.dma_start(out=kpe[:], in_=k_pe_raw.flatten_outer_dims().rearrange("(c p j) r -> p c (j r)", p=P, j=4))
+        w_raw = const.tile([P, 512], BF16, name="w_raw")
+        nc.scalar.dma_start(out=w_raw[:], in_=kv_a_ln_w.partition_broadcast(P))
+
+        s_i = const.tile([P, 16], I32, name="s_i")
+        nc.gpsimd.iota(s_i[:], pattern=[[512, 4], [1, 4]], base=0, channel_multiplier=4)
+        ident_f = const.tile([P, P], F32, name="ident_f")
+        make_identity(nc, ident_f[:])
+        ident_b = const.tile([P, P], BF16, name="ident_b")
+        make_identity(nc, ident_b[:])
+
+        s_f = const.tile([P, 16], F32, name="s_f")
+        nc.vector.tensor_copy(out=s_f[:], in_=s_i[:])
+        fr = const.tile([P, 32], F32, name="fr")
+        nc.vector.memset(fr[:, 0:1], 1.0)
+        for m in range(5):
+            n = 1 << m
+            nc.vector.tensor_scalar(out=fr[:, n:2 * n], in0=fr[:, 0:n], scalar1=THETA ** (-n / 32.0), scalar2=None, op0=ALU.mult)
+        nc.vector.tensor_scalar(out=fr[:], in0=fr[:], scalar1=1.0 / (2.0 * math.pi), scalar2=None, op0=ALU.mult)
+        ang = const.tile([P, 2, 16, 32], F32, name="ang")
+        nc.vector.tensor_tensor(out=ang[:, 0], in0=s_f[:].unsqueeze(2).to_broadcast([P, 16, 32]),
+                                in1=fr[:].unsqueeze(1).to_broadcast([P, 16, 32]), op=ALU.mult)
+        nc.vector.tensor_scalar(out=ang[:, 1], in0=ang[:, 0], scalar1=0.25, scalar2=None, op0=ALU.add)
+        ang_f = ang[:].rearrange("p a s i -> p (a s i)")
+        q_i = const.tile([P, 1024], I32, name="q_i")
+        nc.vector.tensor_copy(out=q_i[:], in_=ang_f)
+        k_f = const.tile([P, 1024], F32, name="k_f")
+        nc.vector.tensor_copy(out=k_f[:], in_=q_i[:])
+        nc.vector.tensor_tensor(out=ang_f, in0=ang_f, in1=k_f[:], op=ALU.subtract)
+        tab = const.tile([P, 2, 16, 32], F32, name="tab")
+        nc.scalar.activation(out=tab[:].rearrange("p a s i -> p (a s i)"), in_=ang_f, func=ACT.Sin, scale=2.0 * math.pi)
+        nsin = const.tile([P, 16, 32], F32, name="nsin")
+        nc.scalar.activation(out=nsin[:], in_=ang[:, 0], func=ACT.Sin, scale=-2.0 * math.pi)
+        eps_t = const.tile([P, 1], F32, name="eps_t")
+        nc.vector.memset(eps_t[:], 1.0)
+        nc.vector.tensor_scalar(out=eps_t[:], in0=eps_t[:], scalar1=EPS, scalar2=None, op0=ALU.mult)
+
+        w_bc = const.tile([P, 4, P], F32, name="w_bc")
+        nc.gpsimd.tensor_copy(out=w_bc[:], in_=w_raw[:].rearrange("p (q a) -> p a q", a=4))
+
+        key_sb = {}
+        v_sb = {}
+        rope = []
+        for b in range(2):
+            x = kpe[:, 4 * b:4 * b + 4, :].rearrange("p c (j h i) -> p (c j) h i", h=2, i=32)
+            ra = const.tile([P, 16, 2, 32], F32, name="ra%d" % b)
+            rb = const.tile([P, 16, 2, 32], F32, name="rb%d" % b)
+            nc.gpsimd.tensor_tensor(out=ra[:], in0=x, in1=tab[:, 1].unsqueeze(2).to_broadcast([P, 16, 2, 32]), op=ALU.mult)
+            nc.gpsimd.tensor_tensor(out=rb[:, :, 0, :], in0=x[:, :, 1, :], in1=nsin[:], op=ALU.mult)
+            nc.gpsimd.tensor_tensor(out=rb[:, :, 1, :], in0=x[:, :, 0, :], in1=tab[:, 0], op=ALU.mult)
+            rope.append((ra, rb))
+
+        def open_chunk(c):
+            key_sb[c] = outp.tile([P, 2, 4, 192], F32, tag="key", name="key")
+            v_sb[c] = outp.tile([P, 2, 4, P], F32, tag="v", name="v")
+            b, cs = divmod(c, 4)
+            ra, rb = rope[b]
+            for h in range(2):
+                nc.gpsimd.tensor_tensor(out=key_sb[c][:, h, :, 128:192],
+                                        in0=ra[:, 4 * cs:4 * cs + 4].rearrange("p j h i -> p j (h i)"),
+                                        in1=rb[:, 4 * cs:4 * cs + 4].rearrange("p j h i -> p j (h i)"), op=ALU.add)
+
+        def word_transposes(xt, words):
+            for g in range(2):
+                for u in range(2):
+                    lo = 256 * g + 128 * u
+                    nc.tensor.transpose(xt[:, g, u, :], words[:, lo:lo + P], ident_f[:])
+
+        wa_grp = const.tile([P, 2, 512, 2], F32, name="wa_grp", align_bytes=64)
+        wa_c = const.tile([P, 2, 512], U32, name="wa_c", align_bytes=64)
+        wa_s = const.tile([P, 2, 512], U8, name="wa_s", align_bytes=64)
+        for a in range(4):
+            xt = xtp.tile([P, 2, 2, P], F32, tag="xt")
+            word_transposes(xt, wa_sb[:, a, :].bitcast(F32))
+            nc.vector.tensor_copy(out=wa_grp[:, :, a * P:(a + 1) * P, :], in_=xt[:].rearrange("p g u r -> p g r u"))
+        for g in range(2):
+            nc.vector.quantize_mx(out=wa_c[:, g, :].bitcast(FP8X4), scales=wa_s[:, g, :],
+                                  in_=wa_grp[:, g].rearrange("p n u -> p (n u)").bitcast(BF16))
+
+        wb_grp = const.tile([P, 512, 2], F32, name="wb_grp", align_bytes=64)
+        wb_c = const.tile([P, 512], U32, name="wb_c", align_bytes=64)
+        wb_s = const.tile([P, 512], U8, name="wb_s", align_bytes=64)
+
+        def prep_wb():
+            for a2 in range(2):
+                xt = xtp.tile([P, 2, 2, P], F32, tag="xt")
+                for a in range(2):
+                    words = wb_sb[:, 2 * a2 + a, :].bitcast(F32).rearrange("p (w u) -> p w u", u=2)
+                    for u in range(2):
+                        nc.tensor.transpose(xt[:, a, u, :], words[:, :, u], ident_f[:])
+                nc.vector.tensor_copy(out=wb_grp[:, a2 * 256:(a2 + 1) * 256, :].rearrange("p (a r) u -> p a r u", a=2),
+                                      in_=xt[:].rearrange("p a u r -> p a r u"))
+            nc.vector.quantize_mx(out=wb_c[:].bitcast(FP8X4), scales=wb_s[:],
+                                  in_=wb_grp[:].rearrange("p n u -> p (n u)").bitcast(BF16))
+
+        grp = {}
+        xtd = {}
+        hcode = {}
+        ck = {}
+        ssq = {}
+        std = {}
+        ckn = {}
+        g2 = {}
+        c2 = {}
+        kv = {}
+
+        def t1(i):
+            grp[i] = work.tile([P, 2, 2, P, 2], F32, tag="grp", name="grp", align_bytes=64)
+            xts = []
+            for s in range(2):
+                c, j = divmod(2 * i + s, 4)
+                xt = xtp.tile([P, 2, 2, P], F32, tag="xt")
+                word_transposes(xt, hs_sb[c][:, j, :].bitcast(F32))
+                xts.append(xt)
+            xtd[i] = xts
+
+        def pass1(i):
+            for s in range(2):
+                nc.vector.tensor_copy(out=grp[i][:, s], in_=xtd[i][s][:].rearrange("p g u r -> p g r u"))
+
+        def quant_hs(i):
+            hc = work.tile([P, 512], U32, tag="hc", name="hc", align_bytes=64)
+            hsc = work.tile([P, 512], U8, tag="hsc", name="hsc", align_bytes=64)
+            nc.vector.quantize_mx(out=hc[:].bitcast(FP8X4), scales=hsc[:],
+                                  in_=grp[i][:].rearrange("p s g r u -> p (s g r u)").bitcast(BF16))
+            hcode[i] = (hc, hsc)
+
+        def s1(i):
+            hc, hsc = hcode[i]
+            ssq[i] = work.tile([P, 2], F32, tag="ssq", name="ssq")
+            cks = []
+            for s in range(2):
+                acc = ckp.tile([P, 512], F32, tag="ck")
+                for g in range(2):
+                    lo = (2 * s + g) * P
+                    nc.tensor.matmul_mx(out=acc[:], lhsT=hc[:, lo:lo + P].bitcast(FP8X4), lhsT_scale=hsc[:, lo:lo + P],
+                                        rhs=wa_c[:, g, :].bitcast(FP8X4), rhs_scale=wa_s[:, g, :],
+                                        start=(g == 0), stop=(g == 1))
+                cks.append(acc)
+            ck[i] = cks
+
+        def square(i):
+            std[i] = work.tile([P, 2], F32, tag="rs", name="rs")
+            for s in range(2):
+                junk = work.tile([P, 512], BF16, tag="junk", name="junk")
+                nc.scalar.activation(out=junk[:], in_=ck[i][s][:], func=ACT.Square, accum_out=ssq[i][:, s:s + 1])
+                nc.scalar.activation(out=std[i][:, s:s + 1], in_=ssq[i][:, s:s + 1], func=ACT.Abs_reciprocal_sqrt,
+                                     scale=1.0 / 512.0, bias=eps_t[:, 0:1])
+
+        def pass3(i):
+            rs = std[i]
+            ckn[i] = work.tile([P, 2, 512], BF16, tag="ckn", name="ckn")
+            for s in range(2):
+                nc.vector.scalar_tensor_tensor(out=ckn[i][:, s, :], in0=ck[i][s][:], scalar=rs[:, s:s + 1],
+                                               in1=w_bc[:].rearrange("p a q -> p (a q)"), op0=ALU.mult, op1=ALU.mult)
+
+        def t2(i):
+            yt = t2p.tile([P, 2, 4, P], BF16, tag="yt")
+            for s in range(2):
+                for a in range(4):
+                    nc.tensor.transpose(yt[:, s, a, :], ckn[i][:, s, a * P:(a + 1) * P], ident_b[:])
+            g2[i] = work.tile([P, 2, P, 4], BF16, tag="g2", name="g2", align_bytes=64)
+            nc.scalar.copy(out=g2[i][:], in_=yt[:].rearrange("p s t r -> p s r t"))
+
+        def quant2(i):
+            cc = work.tile([P, 256], U32, tag="cc", name="cc", align_bytes=64)
+            cs_ = work.tile([P, 256], U8, tag="cs", name="cs_", align_bytes=64)
+            nc.vector.quantize_mx(out=cc[:].bitcast(FP8X4), scales=cs_[:], in_=g2[i][:].rearrange("p s r t -> p (s r t)"))
+            c2[i] = (cc, cs_)
+
+        def s2(i):
+            cc, cs_ = c2[i]
+            kvs = []
+            for s in range(2):
+                acc = kvp.tile([P, 512], F32, tag="kv")
+                nc.tensor.matmul_mx(out=acc[:], lhsT=cc[:, s * P:(s + 1) * P].bitcast(FP8X4), lhsT_scale=cs_[:, s * P:(s + 1) * P],
+                                    rhs=wb_c[:].bitcast(FP8X4), rhs_scale=wb_s[:], start=True, stop=True)
+                kvs.append(acc)
+            kv[i] = kvs
+
+        def pass5(i):
+            for s in range(2):
+                c, j = divmod(2 * i + s, 4)
+                src = kv[i][s][:].rearrange("p (h e d) -> p h e d", h=2, e=2)
+                if i % 2 == 1 and s == 1:
+                    nc.vector.tensor_copy(out=key_sb[c][:, :, j, 0:P], in_=src[:, :, 0, :])
+                    nc.vector.tensor_copy(out=v_sb[c][:, :, j, :], in_=src[:, :, 1, :])
+                else:
+                    nc.scalar.copy(out=key_sb[c][:, :, j, 0:P], in_=src[:, :, 0, :])
+                    nc.scalar.copy(out=v_sb[c][:, :, j, :], in_=src[:, :, 1, :])
+            if i % 2 == 1:
+                c = i // 2
+                b, cs = divmod(c, 4)
+                rows = slice(cs * 512, (cs + 1) * 512)
+                nc.sync.dma_start(out=out_0[b, :, rows, :].rearrange("h (p j) d -> p h (j d)", j=4),
+                                  in_=key_sb[c][:].rearrange("p h j d -> p h (j d)"))
+                nc.sync.dma_start(out=out_1[b, :, rows, :].rearrange("h (p j) d -> p h (j d)", j=4),
+                                  in_=v_sb[c][:].rearrange("p h j d -> p h (j d)"))
+
+        def live(i):
+            return 0 <= i < N_PAIRS
+
+        for it in range(N_PAIRS + 5):
+            if live(it - 2):
+                s1(it - 2)
+                square(it - 2)
+            if live(it - 5):
+                s2(it - 5)
+            if live(it - 1):
+                pass1(it - 1)
+            if live(it - 4):
+                quant2(it - 4)
+            if live(it - 1):
+                quant_hs(it - 1)
+            if it == 1:
+                prep_wb()
+            if live(it - 2):
+                pass3(it - 2)
+            if it % 2 == 0 and 0 <= it // 2 - 1 < 8:
+                open_chunk(it // 2 - 1)
+            if live(it - 5):
+                pass5(it - 5)
+            if live(it - 3):
+                t2(it - 3)
+            if live(it):
+                t1(it)

@@ -1,9 +1,7 @@
 from contextlib import ExitStack
 import math
 
-import concourse.bass as bass
 import concourse.mybir as mybir
-import concourse.tile as tile
 from concourse.masks import make_identity
 
 FLOPS = 2 * 4096 * 1024 * 512 + 2 * 4096 * 512 * 512
@@ -20,14 +18,14 @@ ACT = mybir.ActivationFunctionType
 P = 128
 EPS = 1e-6
 THETA = 10000.0
-N_PAIRS = 16
+N_TILES = 32
 
 
 def tile_modelnew_pb_t_kernel(tc, hidden_states, kv_a_w_ckv, k_pe_raw, kv_a_ln_w, kv_b_w, out_0, out_1):
     nc = tc.nc
     with ExitStack() as ctx:
         const = ctx.enter_context(tc.tile_pool(name="const", bufs=1))
-        work = ctx.enter_context(tc.tile_pool(name="work", bufs=3))
+        work = ctx.enter_context(tc.tile_pool(name="work", bufs=4))
         outp = ctx.enter_context(tc.tile_pool(name="outp", bufs=4))
         xtp = ctx.enter_context(tc.psum_pool(name="xtp", bufs=2))
         ckp = ctx.enter_context(tc.psum_pool(name="ckp", bufs=3))
@@ -35,29 +33,37 @@ def tile_modelnew_pb_t_kernel(tc, hidden_states, kv_a_w_ckv, k_pe_raw, kv_a_ln_w
         kvp = ctx.enter_context(tc.psum_pool(name="kvp", bufs=2))
         ctx.enter_context(tc.manual_schedule())
 
-        hs_v = hidden_states.flatten_outer_dims().rearrange("(c p j) d -> c p (j d)", p=P, j=4)
-        wa_sb = const.tile([P, 4, 1024], BF16, name="wa_sb")
-        nc.sync.dma_start(out=wa_sb[:].rearrange("p a d -> p (a d)"), in_=kv_a_w_ckv.rearrange("(p a) d -> p (a d)", a=4))
-        hs_sb = []
-        for c in range(8):
-            hs_c = const.tile([P, 4, 1024], BF16, name="hs%d" % c)
-            hs_sb.append(hs_c)
-        nc.sync.dma_start(out=hs_sb[0][:].rearrange("p j d -> p (j d)"), in_=hs_v[0])
-        wb_sb = const.tile([P, 4, 512], BF16, name="wb_sb")
-        nc.sync.dma_start(out=wb_sb[:], in_=kv_b_w.rearrange("(a p) k -> p a k", p=P))
-        for c in range(1, 8):
-            nc.sync.dma_start(out=hs_sb[c][:].rearrange("p j d -> p (j d)"), in_=hs_v[c])
-        kpe = const.tile([P, 8, 256], BF16, name="kpe")
-        nc.scalar.dma_start(out=kpe[:], in_=k_pe_raw.flatten_outer_dims().rearrange("(c p j) r -> p c (j r)", p=P, j=4))
-        w_raw = const.tile([P, 512], BF16, name="w_raw")
-        nc.scalar.dma_start(out=w_raw[:], in_=kv_a_ln_w.partition_broadcast(P))
-
         s_i = const.tile([P, 16], I32, name="s_i")
         nc.gpsimd.iota(s_i[:], pattern=[[512, 4], [1, 4]], base=0, channel_multiplier=4)
         ident_f = const.tile([P, P], F32, name="ident_f")
         make_identity(nc, ident_f[:])
+        w_rows = const.tile([P, 512], BF16, name="w_rows")
+        nc.gpsimd.memset(w_rows[:], 0.0)
+        ones_b = const.tile([P, P], BF16, name="ones_b")
+        nc.gpsimd.memset(ones_b[:], 1.0)
         ident_b = const.tile([P, P], BF16, name="ident_b")
         make_identity(nc, ident_b[:])
+
+        hs_v = hidden_states.flatten_outer_dims().rearrange("(c p j) d -> c p (j d)", p=P, j=4)
+        wa_sb = const.tile([P, 4, 1024], BF16, name="wa_sb")
+        wb_sb = const.tile([P, 4, 512], BF16, name="wb_sb")
+        kpe = const.tile([P, 8, 256], BF16, name="kpe")
+        hs_sb = []
+        for c in range(8):
+            hs_c = const.tile([P, 4, 1024], BF16, name="hs%d" % c)
+            hs_sb.append(hs_c)
+
+        def load_hs(c):
+            nc.sync.dma_start(out=hs_sb[c][:].rearrange("p j d -> p (j d)"), in_=hs_v[c])
+
+        nc.sync.dma_start(out=wa_sb[:].rearrange("p a d -> p (a d)"), in_=kv_a_w_ckv.rearrange("(p a) d -> p (a d)", a=4))
+        load_hs(0)
+        nc.sync.dma_start(out=w_rows[0:1, :], in_=kv_a_ln_w.unsqueeze(0))
+        nc.sync.dma_start(out=wb_sb[:], in_=kv_b_w.rearrange("(a p) k -> p a k", p=P))
+        load_hs(1)
+        nc.sync.dma_start(out=kpe[:], in_=k_pe_raw.flatten_outer_dims().rearrange("(c p j) r -> p c (j r)", p=P, j=4))
+        for c in range(2, 8):
+            load_hs(c)
 
         s_f = const.tile([P, 16], F32, name="s_f")
         nc.vector.tensor_copy(out=s_f[:], in_=s_i[:])
@@ -77,38 +83,13 @@ def tile_modelnew_pb_t_kernel(tc, hidden_states, kv_a_w_ckv, k_pe_raw, kv_a_ln_w
         k_f = const.tile([P, 1024], F32, name="k_f")
         nc.vector.tensor_copy(out=k_f[:], in_=q_i[:])
         nc.vector.tensor_tensor(out=ang_f, in0=ang_f, in1=k_f[:], op=ALU.subtract)
+        eps_t = const.tile([P, 1], F32, name="eps_t")
+        nc.vector.memset(eps_t[:], 1.0)
+        nc.vector.tensor_scalar(out=eps_t[:], in0=eps_t[:], scalar1=EPS, scalar2=None, op0=ALU.mult)
         tab = const.tile([P, 2, 16, 32], F32, name="tab")
         nc.scalar.activation(out=tab[:].rearrange("p a s i -> p (a s i)"), in_=ang_f, func=ACT.Sin, scale=2.0 * math.pi)
         nsin = const.tile([P, 16, 32], F32, name="nsin")
         nc.scalar.activation(out=nsin[:], in_=ang[:, 0], func=ACT.Sin, scale=-2.0 * math.pi)
-        eps_t = const.tile([P, 1], F32, name="eps_t")
-        nc.vector.memset(eps_t[:], 1.0)
-        nc.vector.tensor_scalar(out=eps_t[:], in0=eps_t[:], scalar1=EPS, scalar2=None, op0=ALU.mult)
-
-        w_bc = const.tile([P, 4, P], F32, name="w_bc")
-        nc.gpsimd.tensor_copy(out=w_bc[:], in_=w_raw[:].rearrange("p (q a) -> p a q", a=4))
-
-        key_sb = {}
-        v_sb = {}
-        rope = []
-        for b in range(2):
-            x = kpe[:, 4 * b:4 * b + 4, :].rearrange("p c (j h i) -> p (c j) h i", h=2, i=32)
-            ra = const.tile([P, 16, 2, 32], F32, name="ra%d" % b)
-            rb = const.tile([P, 16, 2, 32], F32, name="rb%d" % b)
-            nc.gpsimd.tensor_tensor(out=ra[:], in0=x, in1=tab[:, 1].unsqueeze(2).to_broadcast([P, 16, 2, 32]), op=ALU.mult)
-            nc.gpsimd.tensor_tensor(out=rb[:, :, 0, :], in0=x[:, :, 1, :], in1=nsin[:], op=ALU.mult)
-            nc.gpsimd.tensor_tensor(out=rb[:, :, 1, :], in0=x[:, :, 0, :], in1=tab[:, 0], op=ALU.mult)
-            rope.append((ra, rb))
-
-        def open_chunk(c):
-            key_sb[c] = outp.tile([P, 2, 4, 192], F32, tag="key", name="key")
-            v_sb[c] = outp.tile([P, 2, 4, P], F32, tag="v", name="v")
-            b, cs = divmod(c, 4)
-            ra, rb = rope[b]
-            for h in range(2):
-                nc.gpsimd.tensor_tensor(out=key_sb[c][:, h, :, 128:192],
-                                        in0=ra[:, 4 * cs:4 * cs + 4].rearrange("p j h i -> p j (h i)"),
-                                        in1=rb[:, 4 * cs:4 * cs + 4].rearrange("p j h i -> p j (h i)"), op=ALU.add)
 
         def word_transposes(xt, words):
             for g in range(2):
@@ -122,10 +103,21 @@ def tile_modelnew_pb_t_kernel(tc, hidden_states, kv_a_w_ckv, k_pe_raw, kv_a_ln_w
         for a in range(4):
             xt = xtp.tile([P, 2, 2, P], F32, tag="xt")
             word_transposes(xt, wa_sb[:, a, :].bitcast(F32))
-            nc.vector.tensor_copy(out=wa_grp[:, :, a * P:(a + 1) * P, :], in_=xt[:].rearrange("p g u r -> p g r u"))
+            dst = wa_grp[:, :, a * P:(a + 1) * P, :]
+            if a % 2 == 0:
+                nc.vector.tensor_copy(out=dst, in_=xt[:].rearrange("p g u r -> p g r u"))
+            else:
+                nc.scalar.copy(out=dst, in_=xt[:].rearrange("p g u r -> p g r u"))
         for g in range(2):
             nc.vector.quantize_mx(out=wa_c[:, g, :].bitcast(FP8X4), scales=wa_s[:, g, :],
                                   in_=wa_grp[:, g].rearrange("p n u -> p (n u)").bitcast(BF16))
+
+        w_ps = ckp.tile([P, 512], F32, tag="ck")
+        nc.tensor.matmul(out=w_ps[:], lhsT=ones_b[:], rhs=w_rows[:], start=True, stop=True)
+        w_bc = const.tile([P, 4, P], F32, name="w_bc")
+        nc.scalar.copy(out=w_bc[:], in_=w_ps[:].rearrange("p (q a) -> p a q", a=4))
+        warm = const.tile([P, 1], F32, name="warm")
+        nc.scalar.activation(out=warm[:], in_=eps_t[:], func=ACT.Abs_reciprocal_sqrt)
 
         wb_grp = const.tile([P, 512, 2], F32, name="wb_grp", align_bytes=64)
         wb_c = const.tile([P, 512], U32, name="wb_c", align_bytes=64)
@@ -138,108 +130,109 @@ def tile_modelnew_pb_t_kernel(tc, hidden_states, kv_a_w_ckv, k_pe_raw, kv_a_ln_w
                     words = wb_sb[:, 2 * a2 + a, :].bitcast(F32).rearrange("p (w u) -> p w u", u=2)
                     for u in range(2):
                         nc.tensor.transpose(xt[:, a, u, :], words[:, :, u], ident_f[:])
-                nc.vector.tensor_copy(out=wb_grp[:, a2 * 256:(a2 + 1) * 256, :].rearrange("p (a r) u -> p a r u", a=2),
-                                      in_=xt[:].rearrange("p a u r -> p a r u"))
+                nc.scalar.copy(out=wb_grp[:, a2 * 256:(a2 + 1) * 256, :].rearrange("p (a r) u -> p a r u", a=2),
+                               in_=xt[:].rearrange("p a u r -> p a r u"))
             nc.vector.quantize_mx(out=wb_c[:].bitcast(FP8X4), scales=wb_s[:],
                                   in_=wb_grp[:].rearrange("p n u -> p (n u)").bitcast(BF16))
 
-        grp = {}
         xtd = {}
+        grp = {}
         hcode = {}
         ck = {}
-        ssq = {}
-        std = {}
+        rstd = {}
         ckn = {}
+        ytd = {}
         g2 = {}
         c2 = {}
         kv = {}
+        key_sb = {}
+        v_sb = {}
 
-        def t1(i):
-            grp[i] = work.tile([P, 2, 2, P, 2], F32, tag="grp", name="grp", align_bytes=64)
-            xts = []
-            for s in range(2):
-                c, j = divmod(2 * i + s, 4)
-                xt = xtp.tile([P, 2, 2, P], F32, tag="xt")
-                word_transposes(xt, hs_sb[c][:, j, :].bitcast(F32))
-                xts.append(xt)
-            xtd[i] = xts
+        def open_chunk(c):
+            key_sb[c] = outp.tile([P, 2, 4, 192], F32, tag="key", name="key")
+            v_sb[c] = outp.tile([P, 2, 4, P], F32, tag="v", name="v")
+            cs = c % 4
+            x = kpe[:, c, :].rearrange("p (j h i) -> p j h i", h=2, i=32)
+            rows = slice(4 * cs, 4 * cs + 4)
+            ra = work.tile([P, 4, 2, 32], F32, tag="ra", name="ra")
+            rb = work.tile([P, 4, 2, 32], F32, tag="rb", name="rb")
+            nc.gpsimd.tensor_tensor(out=ra[:], in0=x, in1=tab[:, 1, rows, :].unsqueeze(2).to_broadcast([P, 4, 2, 32]), op=ALU.mult)
+            nc.gpsimd.tensor_tensor(out=rb[:, :, 0, :], in0=x[:, :, 1, :], in1=nsin[:, rows, :], op=ALU.mult)
+            nc.gpsimd.tensor_tensor(out=rb[:, :, 1, :], in0=x[:, :, 0, :], in1=tab[:, 0, rows, :], op=ALU.mult)
+            for h in range(2):
+                nc.gpsimd.tensor_tensor(out=key_sb[c][:, h, :, 128:192], in0=ra[:].rearrange("p j h i -> p j (h i)"),
+                                        in1=rb[:].rearrange("p j h i -> p j (h i)"), op=ALU.add)
 
-        def pass1(i):
-            for s in range(2):
-                nc.vector.tensor_copy(out=grp[i][:, s], in_=xtd[i][s][:].rearrange("p g u r -> p g r u"))
+        def t1(k):
+            c, j = divmod(k, 4)
+            xt = xtp.tile([P, 2, 2, P], F32, tag="xt")
+            word_transposes(xt, hs_sb[c][:, j, :].bitcast(F32))
+            xtd[k] = xt
 
-        def quant_hs(i):
-            hc = work.tile([P, 512], U32, tag="hc", name="hc", align_bytes=64)
-            hsc = work.tile([P, 512], U8, tag="hsc", name="hsc", align_bytes=64)
+        def pass1(k):
+            grp[k] = work.tile([P, 2, P, 2], F32, tag="grp", name="grp", align_bytes=64)
+            nc.vector.tensor_copy(out=grp[k][:], in_=xtd[k][:].rearrange("p g u r -> p g r u"))
+
+        def quant_hs(k):
+            hc = work.tile([P, 256], U32, tag="hc", name="hc", align_bytes=64)
+            hsc = work.tile([P, 256], U8, tag="hsc", name="hsc", align_bytes=64)
             nc.vector.quantize_mx(out=hc[:].bitcast(FP8X4), scales=hsc[:],
-                                  in_=grp[i][:].rearrange("p s g r u -> p (s g r u)").bitcast(BF16))
-            hcode[i] = (hc, hsc)
+                                  in_=grp[k][:].rearrange("p g r u -> p (g r u)").bitcast(BF16))
+            hcode[k] = (hc, hsc)
 
-        def s1(i):
-            hc, hsc = hcode[i]
-            ssq[i] = work.tile([P, 2], F32, tag="ssq", name="ssq")
-            cks = []
-            for s in range(2):
-                acc = ckp.tile([P, 512], F32, tag="ck")
-                for g in range(2):
-                    lo = (2 * s + g) * P
-                    nc.tensor.matmul_mx(out=acc[:], lhsT=hc[:, lo:lo + P].bitcast(FP8X4), lhsT_scale=hsc[:, lo:lo + P],
-                                        rhs=wa_c[:, g, :].bitcast(FP8X4), rhs_scale=wa_s[:, g, :],
-                                        start=(g == 0), stop=(g == 1))
-                cks.append(acc)
-            ck[i] = cks
+        def s1(k):
+            hc, hsc = hcode[k]
+            acc = ckp.tile([P, 512], F32, tag="ck")
+            for g in range(2):
+                nc.tensor.matmul_mx(out=acc[:], lhsT=hc[:, g * P:(g + 1) * P].bitcast(FP8X4), lhsT_scale=hsc[:, g * P:(g + 1) * P],
+                                    rhs=wa_c[:, g, :].bitcast(FP8X4), rhs_scale=wa_s[:, g, :], start=(g == 0), stop=(g == 1))
+            ck[k] = acc
 
-        def square(i):
-            std[i] = work.tile([P, 2], F32, tag="rs", name="rs")
-            for s in range(2):
-                junk = work.tile([P, 512], BF16, tag="junk", name="junk")
-                nc.scalar.activation(out=junk[:], in_=ck[i][s][:], func=ACT.Square, accum_out=ssq[i][:, s:s + 1])
-                nc.scalar.activation(out=std[i][:, s:s + 1], in_=ssq[i][:, s:s + 1], func=ACT.Abs_reciprocal_sqrt,
-                                     scale=1.0 / 512.0, bias=eps_t[:, 0:1])
+        def stats(k):
+            ssq = work.tile([P, 1], F32, tag="ssq", name="ssq")
+            junk = work.tile([P, 512], BF16, tag="junk", name="junk")
+            nc.scalar.activation(out=junk[:], in_=ck[k][:], func=ACT.Square, accum_out=ssq[:])
+            rstd[k] = work.tile([P, 1], F32, tag="rs", name="rs")
+            nc.scalar.activation(out=rstd[k][:], in_=ssq[:], func=ACT.Abs_reciprocal_sqrt, scale=1.0 / 512.0, bias=eps_t[:, 0:1])
 
-        def pass3(i):
-            rs = std[i]
-            ckn[i] = work.tile([P, 2, 512], BF16, tag="ckn", name="ckn")
-            for s in range(2):
-                nc.vector.scalar_tensor_tensor(out=ckn[i][:, s, :], in0=ck[i][s][:], scalar=rs[:, s:s + 1],
-                                               in1=w_bc[:].rearrange("p a q -> p (a q)"), op0=ALU.mult, op1=ALU.mult)
+        def pass3(k):
+            ckn[k] = work.tile([P, 512], BF16, tag="ckn", name="ckn")
+            nc.vector.scalar_tensor_tensor(out=ckn[k][:], in0=ck[k][:], scalar=rstd[k][:, 0:1],
+                                           in1=w_bc[:].rearrange("p a q -> p (a q)"), op0=ALU.mult, op1=ALU.mult)
 
-        def t2(i):
-            yt = t2p.tile([P, 2, 4, P], BF16, tag="yt")
-            for s in range(2):
-                for a in range(4):
-                    nc.tensor.transpose(yt[:, s, a, :], ckn[i][:, s, a * P:(a + 1) * P], ident_b[:])
-            g2[i] = work.tile([P, 2, P, 4], BF16, tag="g2", name="g2", align_bytes=64)
-            nc.scalar.copy(out=g2[i][:], in_=yt[:].rearrange("p s t r -> p s r t"))
+        def t2(k):
+            yt = t2p.tile([P, 4, P], BF16, tag="yt")
+            for a in range(4):
+                nc.tensor.transpose(yt[:, a, :], ckn[k][:, a * P:(a + 1) * P], ident_b[:])
+            ytd[k] = yt
 
-        def quant2(i):
-            cc = work.tile([P, 256], U32, tag="cc", name="cc", align_bytes=64)
-            cs_ = work.tile([P, 256], U8, tag="cs", name="cs_", align_bytes=64)
-            nc.vector.quantize_mx(out=cc[:].bitcast(FP8X4), scales=cs_[:], in_=g2[i][:].rearrange("p s r t -> p (s r t)"))
-            c2[i] = (cc, cs_)
+        def pass4(k):
+            g2[k] = work.tile([P, P, 4], BF16, tag="g2", name="g2", align_bytes=64)
+            nc.scalar.copy(out=g2[k][:], in_=ytd[k][:].rearrange("p t r -> p r t"))
 
-        def s2(i):
-            cc, cs_ = c2[i]
-            kvs = []
-            for s in range(2):
-                acc = kvp.tile([P, 512], F32, tag="kv")
-                nc.tensor.matmul_mx(out=acc[:], lhsT=cc[:, s * P:(s + 1) * P].bitcast(FP8X4), lhsT_scale=cs_[:, s * P:(s + 1) * P],
-                                    rhs=wb_c[:].bitcast(FP8X4), rhs_scale=wb_s[:], start=True, stop=True)
-                kvs.append(acc)
-            kv[i] = kvs
+        def quant2(k):
+            cc = work.tile([P, P], U32, tag="cc", name="cc", align_bytes=64)
+            csc = work.tile([P, P], U8, tag="csc", name="csc", align_bytes=64)
+            nc.vector.quantize_mx(out=cc[:].bitcast(FP8X4), scales=csc[:], in_=g2[k][:].rearrange("p r t -> p (r t)"))
+            c2[k] = (cc, csc)
 
-        def pass5(i):
-            for s in range(2):
-                c, j = divmod(2 * i + s, 4)
-                src = kv[i][s][:].rearrange("p (h e d) -> p h e d", h=2, e=2)
-                if i % 2 == 1 and s == 1:
-                    nc.vector.tensor_copy(out=key_sb[c][:, :, j, 0:P], in_=src[:, :, 0, :])
-                    nc.vector.tensor_copy(out=v_sb[c][:, :, j, :], in_=src[:, :, 1, :])
-                else:
-                    nc.scalar.copy(out=key_sb[c][:, :, j, 0:P], in_=src[:, :, 0, :])
-                    nc.scalar.copy(out=v_sb[c][:, :, j, :], in_=src[:, :, 1, :])
-            if i % 2 == 1:
-                c = i // 2
+        def s2(k):
+            cc, csc = c2[k]
+            acc = kvp.tile([P, 512], F32, tag="kv")
+            nc.tensor.matmul_mx(out=acc[:], lhsT=cc[:].bitcast(FP8X4), lhsT_scale=csc[:],
+                                rhs=wb_c[:].bitcast(FP8X4), rhs_scale=wb_s[:], start=True, stop=True)
+            kv[k] = acc
+
+        def pass5(k):
+            c, j = divmod(k, 4)
+            src = kv[k][:].rearrange("p (h e d) -> p h e d", h=2, e=2)
+            if j == 3:
+                nc.vector.tensor_copy(out=key_sb[c][:, :, j, 0:P], in_=src[:, :, 0, :])
+                nc.vector.tensor_copy(out=v_sb[c][:, :, j, :], in_=src[:, :, 1, :])
+            else:
+                nc.scalar.copy(out=key_sb[c][:, :, j, 0:P], in_=src[:, :, 0, :])
+                nc.scalar.copy(out=v_sb[c][:, :, j, :], in_=src[:, :, 1, :])
+            if j == 3:
                 b, cs = divmod(c, 4)
                 rows = slice(cs * 512, (cs + 1) * 512)
                 nc.sync.dma_start(out=out_0[b, :, rows, :].rearrange("h (p j) d -> p h (j d)", j=4),
@@ -247,30 +240,32 @@ def tile_modelnew_pb_t_kernel(tc, hidden_states, kv_a_w_ckv, k_pe_raw, kv_a_ln_w
                 nc.sync.dma_start(out=out_1[b, :, rows, :].rearrange("h (p j) d -> p h (j d)", j=4),
                                   in_=v_sb[c][:].rearrange("p h j d -> p h (j d)"))
 
-        def live(i):
-            return 0 <= i < N_PAIRS
+        def live(k):
+            return 0 <= k < N_TILES
 
-        for it in range(N_PAIRS + 5):
-            if live(it - 2):
-                s1(it - 2)
-                square(it - 2)
-            if live(it - 5):
-                s2(it - 5)
-            if live(it - 1):
-                pass1(it - 1)
-            if live(it - 4):
-                quant2(it - 4)
-            if live(it - 1):
-                quant_hs(it - 1)
-            if it == 1:
+        for r in range(N_TILES + 9):
+            if live(r - 6):
+                pass4(r - 6)
+            if live(r - 3):
+                s1(r - 3)
+                stats(r - 3)
+            if live(r - 8):
+                s2(r - 8)
+            if live(r - 4):
+                pass3(r - 4)
+            if live(r - 1):
+                pass1(r - 1)
+            if live(r - 2):
+                quant_hs(r - 2)
+            if live(r - 7):
+                quant2(r - 7)
+            if r == 4:
                 prep_wb()
-            if live(it - 2):
-                pass3(it - 2)
-            if it % 2 == 0 and 0 <= it // 2 - 1 < 8:
-                open_chunk(it // 2 - 1)
-            if live(it - 5):
-                pass5(it - 5)
-            if live(it - 3):
-                t2(it - 3)
-            if live(it):
-                t1(it)
+            if r % 4 == 0 and r // 4 < 8:
+                open_chunk(r // 4)
+            if live(r - 8):
+                pass5(r - 8)
+            if live(r - 5):
+                t2(r - 5)
+            if live(r):
+                t1(r)

@@ -25,24 +25,16 @@ def tile_modelnew_pb_t_kernel(tc, hidden_states, kv_a_w_ckv, k_pe_raw, kv_a_ln_w
     nc = tc.nc
     with ExitStack() as ctx:
         const = ctx.enter_context(tc.tile_pool(name="const", bufs=1))
-        work = ctx.enter_context(tc.tile_pool(name="work", bufs=4))
+        work = ctx.enter_context(tc.tile_pool(name="work", bufs=6))
         outp = ctx.enter_context(tc.tile_pool(name="outp", bufs=4))
-        xtp = ctx.enter_context(tc.psum_pool(name="xtp", bufs=2))
-        ckp = ctx.enter_context(tc.psum_pool(name="ckp", bufs=3))
-        t2p = ctx.enter_context(tc.psum_pool(name="t2p", bufs=1))
-        kvp = ctx.enter_context(tc.psum_pool(name="kvp", bufs=2))
+        tpp = ctx.enter_context(tc.psum_pool(name="tpp", bufs=4))
+        mxp = ctx.enter_context(tc.psum_pool(name="mxp", bufs=4))
         ctx.enter_context(tc.manual_schedule())
 
         s_i = const.tile([P, 16], I32, name="s_i")
         nc.gpsimd.iota(s_i[:], pattern=[[512, 4], [1, 4]], base=0, channel_multiplier=4)
         ident_f = const.tile([P, P], F32, name="ident_f")
         make_identity(nc, ident_f[:])
-        w_rows = const.tile([P, 512], BF16, name="w_rows")
-        nc.gpsimd.memset(w_rows[:], 0.0)
-        ones_b = const.tile([P, P], BF16, name="ones_b")
-        nc.gpsimd.memset(ones_b[:], 1.0)
-        ident_b = const.tile([P, P], BF16, name="ident_b")
-        make_identity(nc, ident_b[:])
 
         hs_v = hidden_states.flatten_outer_dims().rearrange("(c p j) d -> c p (j d)", p=P, j=4)
         wa_sb = const.tile([P, 4, 1024], BF16, name="wa_sb")
@@ -58,7 +50,8 @@ def tile_modelnew_pb_t_kernel(tc, hidden_states, kv_a_w_ckv, k_pe_raw, kv_a_ln_w
 
         nc.sync.dma_start(out=wa_sb[:].rearrange("p a d -> p (a d)"), in_=kv_a_w_ckv.rearrange("(p a) d -> p (a d)", a=4))
         load_hs(0)
-        nc.sync.dma_start(out=w_rows[0:1, :], in_=kv_a_ln_w.unsqueeze(0))
+        w_pt = const.tile([P, 4], BF16, name="w_pt")
+        nc.sync.dma_start(out=w_pt[:], in_=kv_a_ln_w.rearrange("(p t) -> p t", t=4))
         nc.sync.dma_start(out=wb_sb[:], in_=kv_b_w.rearrange("(a p) k -> p a k", p=P))
         load_hs(1)
         nc.sync.dma_start(out=kpe[:], in_=k_pe_raw.flatten_outer_dims().rearrange("(c p j) r -> p c (j r)", p=P, j=4))
@@ -101,7 +94,7 @@ def tile_modelnew_pb_t_kernel(tc, hidden_states, kv_a_w_ckv, k_pe_raw, kv_a_ln_w
         wa_c = const.tile([P, 2, 512], U32, name="wa_c", align_bytes=64)
         wa_s = const.tile([P, 2, 512], U8, name="wa_s", align_bytes=64)
         for a in range(4):
-            xt = xtp.tile([P, 2, 2, P], F32, tag="xt")
+            xt = tpp.tile([P, 2, 2, P], F32, tag="tp")
             word_transposes(xt, wa_sb[:, a, :].bitcast(F32))
             dst = wa_grp[:, :, a * P:(a + 1) * P, :]
             if a % 2 == 0:
@@ -112,10 +105,6 @@ def tile_modelnew_pb_t_kernel(tc, hidden_states, kv_a_w_ckv, k_pe_raw, kv_a_ln_w
             nc.vector.quantize_mx(out=wa_c[:, g, :].bitcast(FP8X4), scales=wa_s[:, g, :],
                                   in_=wa_grp[:, g].rearrange("p n u -> p (n u)").bitcast(BF16))
 
-        w_ps = ckp.tile([P, 512], F32, tag="ck")
-        nc.tensor.matmul(out=w_ps[:], lhsT=ones_b[:], rhs=w_rows[:], start=True, stop=True)
-        w_bc = const.tile([P, 4, P], F32, name="w_bc")
-        nc.scalar.copy(out=w_bc[:], in_=w_ps[:].rearrange("p (q a) -> p a q", a=4))
         warm = const.tile([P, 1], F32, name="warm")
         nc.scalar.activation(out=warm[:], in_=eps_t[:], func=ACT.Abs_reciprocal_sqrt)
 
@@ -125,13 +114,15 @@ def tile_modelnew_pb_t_kernel(tc, hidden_states, kv_a_w_ckv, k_pe_raw, kv_a_ln_w
 
         def prep_wb():
             for a2 in range(2):
-                xt = xtp.tile([P, 2, 2, P], F32, tag="xt")
+                xt = tpp.tile([P, 2, 2, P], F32, tag="tp")
                 for a in range(2):
                     words = wb_sb[:, 2 * a2 + a, :].bitcast(F32).rearrange("p (w u) -> p w u", u=2)
                     for u in range(2):
                         nc.tensor.transpose(xt[:, a, u, :], words[:, :, u], ident_f[:])
                 nc.scalar.copy(out=wb_grp[:, a2 * 256:(a2 + 1) * 256, :].rearrange("p (a r) u -> p a r u", a=2),
                                in_=xt[:].rearrange("p a u r -> p a r u"))
+
+        def quant_wb():
             nc.vector.quantize_mx(out=wb_c[:].bitcast(FP8X4), scales=wb_s[:],
                                   in_=wb_grp[:].rearrange("p n u -> p (n u)").bitcast(BF16))
 
@@ -165,7 +156,7 @@ def tile_modelnew_pb_t_kernel(tc, hidden_states, kv_a_w_ckv, k_pe_raw, kv_a_ln_w
 
         def t1(k):
             c, j = divmod(k, 4)
-            xt = xtp.tile([P, 2, 2, P], F32, tag="xt")
+            xt = tpp.tile([P, 2, 2, P], F32, tag="tp")
             word_transposes(xt, hs_sb[c][:, j, :].bitcast(F32))
             xtd[k] = xt
 
@@ -182,7 +173,7 @@ def tile_modelnew_pb_t_kernel(tc, hidden_states, kv_a_w_ckv, k_pe_raw, kv_a_ln_w
 
         def s1(k):
             hc, hsc = hcode[k]
-            acc = ckp.tile([P, 512], F32, tag="ck")
+            acc = mxp.tile([P, 512], F32, tag="mx")
             for g in range(2):
                 nc.tensor.matmul_mx(out=acc[:], lhsT=hc[:, g * P:(g + 1) * P].bitcast(FP8X4), lhsT_scale=hsc[:, g * P:(g + 1) * P],
                                     rhs=wa_c[:, g, :].bitcast(FP8X4), rhs_scale=wa_s[:, g, :], start=(g == 0), stop=(g == 1))
@@ -195,20 +186,19 @@ def tile_modelnew_pb_t_kernel(tc, hidden_states, kv_a_w_ckv, k_pe_raw, kv_a_ln_w
             rstd[k] = work.tile([P, 1], F32, tag="rs", name="rs")
             nc.scalar.activation(out=rstd[k][:], in_=ssq[:], func=ACT.Abs_reciprocal_sqrt, scale=1.0 / 512.0, bias=eps_t[:, 0:1])
 
-        def pass3(k):
-            ckn[k] = work.tile([P, 512], BF16, tag="ckn", name="ckn")
-            nc.vector.scalar_tensor_tensor(out=ckn[k][:], in0=ck[k][:], scalar=rstd[k][:, 0:1],
-                                           in1=w_bc[:].rearrange("p a q -> p (a q)"), op0=ALU.mult, op1=ALU.mult)
+            ckn[k] = work.tile([P, 512], F32, tag="ckn", name="ckn")
+            nc.scalar.activation(out=ckn[k][:], in_=ck[k][:], func=ACT.Copy, scale=rstd[k][:, 0:1])
 
         def t2(k):
-            yt = t2p.tile([P, 4, P], BF16, tag="yt")
+            yt = tpp.tile([P, 4, P], F32, tag="tp")
             for a in range(4):
-                nc.tensor.transpose(yt[:, a, :], ckn[k][:, a * P:(a + 1) * P], ident_b[:])
+                nc.tensor.transpose(yt[:, a, :], ckn[k][:, a * P:(a + 1) * P], ident_f[:])
             ytd[k] = yt
 
         def pass4(k):
             g2[k] = work.tile([P, P, 4], BF16, tag="g2", name="g2", align_bytes=64)
-            nc.scalar.copy(out=g2[k][:], in_=ytd[k][:].rearrange("p t r -> p r t"))
+            nc.vector.tensor_tensor(out=g2[k][:], in0=ytd[k][:].rearrange("p t r -> p r t"),
+                                    in1=w_pt[:].unsqueeze(1).to_broadcast([P, P, 4]), op=ALU.mult)
 
         def quant2(k):
             cc = work.tile([P, P], U32, tag="cc", name="cc", align_bytes=64)
@@ -218,7 +208,7 @@ def tile_modelnew_pb_t_kernel(tc, hidden_states, kv_a_w_ckv, k_pe_raw, kv_a_ln_w
 
         def s2(k):
             cc, csc = c2[k]
-            acc = kvp.tile([P, 512], F32, tag="kv")
+            acc = mxp.tile([P, 512], F32, tag="mx")
             nc.tensor.matmul_mx(out=acc[:], lhsT=cc[:].bitcast(FP8X4), lhsT_scale=csc[:],
                                 rhs=wb_c[:].bitcast(FP8X4), rhs_scale=wb_s[:], start=True, stop=True)
             kv[k] = acc
@@ -243,29 +233,30 @@ def tile_modelnew_pb_t_kernel(tc, hidden_states, kv_a_w_ckv, k_pe_raw, kv_a_ln_w
         def live(k):
             return 0 <= k < N_TILES
 
-        for r in range(N_TILES + 9):
-            if live(r - 6):
-                pass4(r - 6)
-            if live(r - 3):
-                s1(r - 3)
-                stats(r - 3)
-            if live(r - 8):
-                s2(r - 8)
-            if live(r - 4):
-                pass3(r - 4)
-            if live(r - 1):
-                pass1(r - 1)
+        for r in range(N_TILES + 14):
+            if r == 3:
+                prep_wb()
+            if r == 7:
+                quant_wb()
+            if live(r - 10):
+                quant2(r - 10)
             if live(r - 2):
                 quant_hs(r - 2)
-            if live(r - 7):
-                quant2(r - 7)
-            if r == 4:
-                prep_wb()
-            if r % 4 == 0 and r // 4 < 8:
-                open_chunk(r // 4)
-            if live(r - 8):
-                pass5(r - 8)
+            if r % 4 == 0 and 0 <= r // 4 - 1 < 8:
+                open_chunk(r // 4 - 1)
+            if live(r - 13):
+                pass5(r - 13)
+            if live(r - 1):
+                pass1(r - 1)
+            if live(r - 12):
+                s2(r - 12)
+            if live(r - 4):
+                s1(r - 4)
             if live(r - 5):
-                t2(r - 5)
+                stats(r - 5)
+            if live(r - 8):
+                pass4(r - 8)
             if live(r):
                 t1(r)
+            if live(r - 7):
+                t2(r - 7)

@@ -33,6 +33,8 @@ def tile_modelnew_pb_t_kernel(tc, hidden_states, kv_a_w_ckv, k_pe_raw, kv_a_ln_w
 
         s_i = const.tile([P, 16], I32, name="s_i")
         nc.gpsimd.iota(s_i[:], pattern=[[512, 4], [1, 4]], base=0, channel_multiplier=4)
+        zeros = const.tile([P, 512], BF16, name="zeros")
+        nc.vector.memset(zeros[:], 0.0)
         ident_f = const.tile([P, P], F32, name="ident_f")
         make_identity(nc, ident_f[:])
 
@@ -84,6 +86,21 @@ def tile_modelnew_pb_t_kernel(tc, hidden_states, kv_a_w_ckv, k_pe_raw, kv_a_ln_w
         nsin = const.tile([P, 16, 32], F32, name="nsin")
         nc.scalar.activation(out=nsin[:], in_=ang[:, 0], func=ACT.Sin, scale=-2.0 * math.pi)
 
+        def plain_filler(passes):
+            acc = mxp.tile([P, 512], F32, tag="mx")
+            for i in range(passes):
+                nc.tensor.matmul(out=acc[:], lhsT=zeros[:, 0:P], rhs=zeros[:], start=(i == 0), stop=(i == passes - 1))
+
+        def mx_filler(passes):
+            acc = mxp.tile([P, 512], F32, tag="mx")
+            for i in range(passes):
+                nc.tensor.matmul_mx(out=acc[:], lhsT=wa_c[:, 0, 0:P].bitcast(FP8X4), lhsT_scale=wa_s[:, 0, 0:P],
+                                    rhs=wa_c[:, 0, :].bitcast(FP8X4), rhs_scale=wa_s[:, 0, :],
+                                    start=(i == 0), stop=(i == passes - 1))
+
+        plain_filler(5)
+        plain_filler(5)
+
         def word_transposes(xt, words):
             for g in range(2):
                 for u in range(2):
@@ -101,6 +118,7 @@ def tile_modelnew_pb_t_kernel(tc, hidden_states, kv_a_w_ckv, k_pe_raw, kv_a_ln_w
                 nc.vector.tensor_copy(out=dst, in_=xt[:].rearrange("p g u r -> p g r u"))
             else:
                 nc.scalar.copy(out=dst, in_=xt[:].rearrange("p g u r -> p g r u"))
+            plain_filler(1)
         for g in range(2):
             nc.vector.quantize_mx(out=wa_c[:, g, :].bitcast(FP8X4), scales=wa_s[:, g, :],
                                   in_=wa_grp[:, g].rearrange("p n u -> p (n u)").bitcast(BF16))
@@ -250,8 +268,16 @@ def tile_modelnew_pb_t_kernel(tc, hidden_states, kv_a_w_ckv, k_pe_raw, kv_a_ln_w
                 pass1(r - 1)
             if live(r - 12):
                 s2(r - 12)
+            elif r < 3:
+                plain_filler(1)
+            elif r < 12:
+                mx_filler(1)
             if live(r - 4):
                 s1(r - 4)
+            elif r < 3:
+                plain_filler(2)
+            elif r < 4:
+                mx_filler(2)
             if live(r - 5):
                 stats(r - 5)
             if live(r - 8):

@@ -27,14 +27,12 @@ def tile_modelnew_pb_t_kernel(tc, hidden_states, kv_a_w_ckv, k_pe_raw, kv_a_ln_w
         const = ctx.enter_context(tc.tile_pool(name="const", bufs=1))
         work = ctx.enter_context(tc.tile_pool(name="work", bufs=6))
         outp = ctx.enter_context(tc.tile_pool(name="outp", bufs=4))
-        tpp = ctx.enter_context(tc.psum_pool(name="tpp", bufs=4))
-        mxp = ctx.enter_context(tc.psum_pool(name="mxp", bufs=4))
+        tpp = ctx.enter_context(tc.psum_pool(name="tpp", bufs=3))
+        mxp = ctx.enter_context(tc.psum_pool(name="mxp", bufs=5))
         ctx.enter_context(tc.manual_schedule())
 
         s_i = const.tile([P, 16], I32, name="s_i")
         nc.gpsimd.iota(s_i[:], pattern=[[512, 4], [1, 4]], base=0, channel_multiplier=4)
-        zeros = const.tile([P, 512], BF16, name="zeros")
-        nc.vector.memset(zeros[:], 0.0)
         ident_f = const.tile([P, P], F32, name="ident_f")
         make_identity(nc, ident_f[:])
 
@@ -86,21 +84,6 @@ def tile_modelnew_pb_t_kernel(tc, hidden_states, kv_a_w_ckv, k_pe_raw, kv_a_ln_w
         nsin = const.tile([P, 16, 32], F32, name="nsin")
         nc.scalar.activation(out=nsin[:], in_=ang[:, 0], func=ACT.Sin, scale=-2.0 * math.pi)
 
-        def plain_filler(passes):
-            acc = mxp.tile([P, 512], F32, tag="mx")
-            for i in range(passes):
-                nc.tensor.matmul(out=acc[:], lhsT=zeros[:, 0:P], rhs=zeros[:], start=(i == 0), stop=(i == passes - 1))
-
-        def mx_filler(passes):
-            acc = mxp.tile([P, 512], F32, tag="mx")
-            for i in range(passes):
-                nc.tensor.matmul_mx(out=acc[:], lhsT=wa_c[:, 0, 0:P].bitcast(FP8X4), lhsT_scale=wa_s[:, 0, 0:P],
-                                    rhs=wa_c[:, 0, :].bitcast(FP8X4), rhs_scale=wa_s[:, 0, :],
-                                    start=(i == 0), stop=(i == passes - 1))
-
-        plain_filler(5)
-        plain_filler(5)
-
         def word_transposes(xt, words):
             for g in range(2):
                 for u in range(2):
@@ -118,7 +101,6 @@ def tile_modelnew_pb_t_kernel(tc, hidden_states, kv_a_w_ckv, k_pe_raw, kv_a_ln_w
                 nc.vector.tensor_copy(out=dst, in_=xt[:].rearrange("p g u r -> p g r u"))
             else:
                 nc.scalar.copy(out=dst, in_=xt[:].rearrange("p g u r -> p g r u"))
-            plain_filler(1)
         for g in range(2):
             nc.vector.quantize_mx(out=wa_c[:, g, :].bitcast(FP8X4), scales=wa_s[:, g, :],
                                   in_=wa_grp[:, g].rearrange("p n u -> p (n u)").bitcast(BF16))
@@ -130,15 +112,14 @@ def tile_modelnew_pb_t_kernel(tc, hidden_states, kv_a_w_ckv, k_pe_raw, kv_a_ln_w
         wb_c = const.tile([P, 512], U32, name="wb_c", align_bytes=64)
         wb_s = const.tile([P, 512], U8, name="wb_s", align_bytes=64)
 
-        def prep_wb():
-            for a2 in range(2):
-                xt = tpp.tile([P, 2, 2, P], F32, tag="tp")
-                for a in range(2):
-                    words = wb_sb[:, 2 * a2 + a, :].bitcast(F32).rearrange("p (w u) -> p w u", u=2)
-                    for u in range(2):
-                        nc.tensor.transpose(xt[:, a, u, :], words[:, :, u], ident_f[:])
-                nc.scalar.copy(out=wb_grp[:, a2 * 256:(a2 + 1) * 256, :].rearrange("p (a r) u -> p a r u", a=2),
-                               in_=xt[:].rearrange("p a u r -> p a r u"))
+        def prep_wb(a2):
+            xt = tpp.tile([P, 2, 2, P], F32, tag="tp")
+            for a in range(2):
+                words = wb_sb[:, 2 * a2 + a, :].bitcast(F32).rearrange("p (w u) -> p w u", u=2)
+                for u in range(2):
+                    nc.tensor.transpose(xt[:, a, u, :], words[:, :, u], ident_f[:])
+            nc.scalar.copy(out=wb_grp[:, a2 * 256:(a2 + 1) * 256, :].rearrange("p (a r) u -> p a r u", a=2),
+                           in_=xt[:].rearrange("p a u r -> p a r u"))
 
         def quant_wb():
             nc.vector.quantize_mx(out=wb_c[:].bitcast(FP8X4), scales=wb_s[:],
@@ -149,6 +130,7 @@ def tile_modelnew_pb_t_kernel(tc, hidden_states, kv_a_w_ckv, k_pe_raw, kv_a_ln_w
         hcode = {}
         ck = {}
         rstd = {}
+        ssq = {}
         ckn = {}
         ytd = {}
         g2 = {}
@@ -197,13 +179,16 @@ def tile_modelnew_pb_t_kernel(tc, hidden_states, kv_a_w_ckv, k_pe_raw, kv_a_ln_w
                                     rhs=wa_c[:, g, :].bitcast(FP8X4), rhs_scale=wa_s[:, g, :], start=(g == 0), stop=(g == 1))
             ck[k] = acc
 
-        def stats(k):
-            ssq = work.tile([P, 1], F32, tag="ssq", name="ssq")
+        def square(k):
+            ssq[k] = work.tile([P, 1], F32, tag="ssq", name="ssq")
             junk = work.tile([P, 512], BF16, tag="junk", name="junk")
-            nc.scalar.activation(out=junk[:], in_=ck[k][:], func=ACT.Square, accum_out=ssq[:])
-            rstd[k] = work.tile([P, 1], F32, tag="rs", name="rs")
-            nc.scalar.activation(out=rstd[k][:], in_=ssq[:], func=ACT.Abs_reciprocal_sqrt, scale=1.0 / 512.0, bias=eps_t[:, 0:1])
+            nc.scalar.activation(out=junk[:], in_=ck[k][:], func=ACT.Square, accum_out=ssq[k][:])
 
+        def rsqrt(k):
+            rstd[k] = work.tile([P, 1], F32, tag="rs", name="rs")
+            nc.scalar.activation(out=rstd[k][:], in_=ssq[k][:], func=ACT.Abs_reciprocal_sqrt, scale=1.0 / 512.0, bias=eps_t[:, 0:1])
+
+        def pass3(k):
             ckn[k] = work.tile([P, 512], F32, tag="ckn", name="ckn")
             nc.scalar.activation(out=ckn[k][:], in_=ck[k][:], func=ACT.Copy, scale=rstd[k][:, 0:1])
 
@@ -252,37 +237,33 @@ def tile_modelnew_pb_t_kernel(tc, hidden_states, kv_a_w_ckv, k_pe_raw, kv_a_ln_w
             return 0 <= k < N_TILES
 
         for r in range(N_TILES + 14):
-            if r == 3:
-                prep_wb()
-            if r == 7:
-                quant_wb()
-            if live(r - 10):
-                quant2(r - 10)
-            if live(r - 2):
-                quant_hs(r - 2)
             if r % 4 == 0 and 0 <= r // 4 - 1 < 8:
                 open_chunk(r // 4 - 1)
+            if r == 7:
+                quant_wb()
             if live(r - 13):
                 pass5(r - 13)
-            if live(r - 1):
-                pass1(r - 1)
+            if live(r - 8):
+                t2(r - 8)
+            elif r == 3 or r == 4:
+                prep_wb(r - 3)
             if live(r - 12):
                 s2(r - 12)
-            elif r < 3:
-                plain_filler(1)
-            elif r < 12:
-                mx_filler(1)
+            if live(r - 10):
+                quant2(r - 10)
             if live(r - 4):
                 s1(r - 4)
-            elif r < 3:
-                plain_filler(2)
-            elif r < 4:
-                mx_filler(2)
+            if live(r - 3):
+                quant_hs(r - 3)
             if live(r - 5):
-                stats(r - 5)
-            if live(r - 8):
-                pass4(r - 8)
+                square(r - 5)
+            if live(r - 6):
+                pass3(r - 6)
+            if live(r - 5):
+                rsqrt(r - 5)
             if live(r):
                 t1(r)
-            if live(r - 7):
-                t2(r - 7)
+            if live(r - 1):
+                pass1(r - 1)
+            if live(r - 8):
+                pass4(r - 8)

@@ -36,19 +36,30 @@ def tile_modelnew_pb_t_kernel(tc, hidden_states, kv_a_w_ckv, k_pe_raw, kv_a_ln_w
         ident_f = const.tile([P, P], F32, name="ident_f")
         make_identity(nc, ident_f[:])
 
+        one = const.tile([P, 1], F32, name="one")
+        nc.vector.memset(one[:], 1.0)
+        warm0 = const.tile([P, 1], F32, name="warm0")
+        nc.scalar.activation(out=warm0[:], in_=one[:], func=ACT.Sin)
+
         hs_v = hidden_states.flatten_outer_dims().rearrange("(c p j) d -> c p (j d)", p=P, j=4)
-        wa_sb = const.tile([P, 4, 1024], BF16, name="wa_sb")
+        wa_sb = []
+        for a in range(4):
+            wa_a = const.tile([P, 1024], BF16, name="wa%d" % a)
+            wa_sb.append(wa_a)
         wb_sb = const.tile([P, 4, 512], BF16, name="wb_sb")
         kpe = const.tile([P, 8, 256], BF16, name="kpe")
         hs_sb = []
-        for c in range(8):
-            hs_c = const.tile([P, 4, 1024], BF16, name="hs%d" % c)
+        for h2 in range(16):
+            hs_c = const.tile([P, 2, 1024], BF16, name="hs%d" % h2)
             hs_sb.append(hs_c)
 
         def load_hs(c):
-            nc.sync.dma_start(out=hs_sb[c][:].rearrange("p j d -> p (j d)"), in_=hs_v[c])
+            for e in range(2):
+                nc.sync.dma_start(out=hs_sb[2 * c + e][:].rearrange("p j d -> p (j d)"), in_=hs_v[c][:, e * 2048:(e + 1) * 2048])
 
-        nc.sync.dma_start(out=wa_sb[:].rearrange("p a d -> p (a d)"), in_=kv_a_w_ckv.rearrange("(p a) d -> p (a d)", a=4))
+        wa_v = kv_a_w_ckv.rearrange("(p a) d -> a p d", a=4)
+        for a in range(4):
+            nc.sync.dma_start(out=wa_sb[a][:], in_=wa_v[a])
         load_hs(0)
         w_pt = const.tile([P, 4], BF16, name="w_pt")
         nc.sync.dma_start(out=w_pt[:], in_=kv_a_ln_w.rearrange("(p t) -> p t", t=4))
@@ -80,9 +91,7 @@ def tile_modelnew_pb_t_kernel(tc, hidden_states, kv_a_w_ckv, k_pe_raw, kv_a_ln_w
         nc.vector.memset(eps_t[:], 1.0)
         nc.vector.tensor_scalar(out=eps_t[:], in0=eps_t[:], scalar1=EPS, scalar2=None, op0=ALU.mult)
         tab = const.tile([P, 2, 16, 32], F32, name="tab")
-        nc.scalar.activation(out=tab[:].rearrange("p a s i -> p (a s i)"), in_=ang_f, func=ACT.Sin, scale=2.0 * math.pi)
         nsin = const.tile([P, 16, 32], F32, name="nsin")
-        nc.scalar.activation(out=nsin[:], in_=ang[:, 0], func=ACT.Sin, scale=-2.0 * math.pi)
 
         def word_transposes(xt, words):
             for g in range(2):
@@ -95,18 +104,19 @@ def tile_modelnew_pb_t_kernel(tc, hidden_states, kv_a_w_ckv, k_pe_raw, kv_a_ln_w
         wa_s = const.tile([P, 2, 512], U8, name="wa_s", align_bytes=64)
         for a in range(4):
             xt = tpp.tile([P, 2, 2, P], F32, tag="tp")
-            word_transposes(xt, wa_sb[:, a, :].bitcast(F32))
+            word_transposes(xt, wa_sb[a][:].bitcast(F32))
             dst = wa_grp[:, :, a * P:(a + 1) * P, :]
-            if a % 2 == 0:
-                nc.vector.tensor_copy(out=dst, in_=xt[:].rearrange("p g u r -> p g r u"))
-            else:
+            if a < 2:
                 nc.scalar.copy(out=dst, in_=xt[:].rearrange("p g u r -> p g r u"))
+            else:
+                nc.vector.tensor_copy(out=dst, in_=xt[:].rearrange("p g u r -> p g r u"))
+        nc.scalar.activation(out=tab[:].rearrange("p a s i -> p (a s i)"), in_=ang_f, func=ACT.Sin, scale=2.0 * math.pi)
+        nc.scalar.activation(out=nsin[:], in_=ang[:, 0], func=ACT.Sin, scale=-2.0 * math.pi)
         for g in range(2):
             nc.vector.quantize_mx(out=wa_c[:, g, :].bitcast(FP8X4), scales=wa_s[:, g, :],
                                   in_=wa_grp[:, g].rearrange("p n u -> p (n u)").bitcast(BF16))
 
         warm = const.tile([P, 1], F32, name="warm")
-        nc.scalar.activation(out=warm[:], in_=eps_t[:], func=ACT.Abs_reciprocal_sqrt)
 
         wb_grp = const.tile([P, 512, 2], F32, name="wb_grp", align_bytes=64)
         wb_c = const.tile([P, 512], U32, name="wb_c", align_bytes=64)
@@ -155,14 +165,16 @@ def tile_modelnew_pb_t_kernel(tc, hidden_states, kv_a_w_ckv, k_pe_raw, kv_a_ln_w
                                         in1=rb[:].rearrange("p j h i -> p j (h i)"), op=ALU.add)
 
         def t1(k):
-            c, j = divmod(k, 4)
             xt = tpp.tile([P, 2, 2, P], F32, tag="tp")
-            word_transposes(xt, hs_sb[c][:, j, :].bitcast(F32))
+            word_transposes(xt, hs_sb[k // 2][:, k % 2, :].bitcast(F32))
             xtd[k] = xt
 
         def pass1(k):
             grp[k] = work.tile([P, 2, P, 2], F32, tag="grp", name="grp", align_bytes=64)
-            nc.vector.tensor_copy(out=grp[k][:], in_=xtd[k][:].rearrange("p g u r -> p g r u"))
+            if k < 2:
+                nc.scalar.copy(out=grp[k][:], in_=xtd[k][:].rearrange("p g u r -> p g r u"))
+            else:
+                nc.vector.tensor_copy(out=grp[k][:], in_=xtd[k][:].rearrange("p g u r -> p g r u"))
 
         def quant_hs(k):
             hc = work.tile([P, 256], U32, tag="hc", name="hc", align_bytes=64)
@@ -225,9 +237,12 @@ def tile_modelnew_pb_t_kernel(tc, hidden_states, kv_a_w_ckv, k_pe_raw, kv_a_ln_w
             else:
                 nc.scalar.copy(out=key_sb[c][:, :, j, 0:P], in_=src[:, :, 0, :])
                 nc.scalar.copy(out=v_sb[c][:, :, j, :], in_=src[:, :, 1, :])
-            if j == 3:
-                b, cs = divmod(c, 4)
-                rows = slice(cs * 512, (cs + 1) * 512)
+            b, cs = divmod(c, 4)
+            rows = slice(cs * 512, (cs + 1) * 512)
+            if c == 7:
+                nc.sync.dma_start(out=out_0[b, :, rows, :].rearrange("h (p j) d -> j p h d", j=4)[j], in_=key_sb[c][:, :, j, :])
+                nc.sync.dma_start(out=out_1[b, :, rows, :].rearrange("h (p j) d -> j p h d", j=4)[j], in_=v_sb[c][:, :, j, :])
+            elif j == 3:
                 nc.sync.dma_start(out=out_0[b, :, rows, :].rearrange("h (p j) d -> p h (j d)", j=4),
                                   in_=key_sb[c][:].rearrange("p h j d -> p h (j d)"))
                 nc.sync.dma_start(out=out_1[b, :, rows, :].rearrange("h (p j) d -> p h (j d)", j=4),
@@ -265,5 +280,7 @@ def tile_modelnew_pb_t_kernel(tc, hidden_states, kv_a_w_ckv, k_pe_raw, kv_a_ln_w
                 t1(r)
             if live(r - 1):
                 pass1(r - 1)
+            if r == 2:
+                nc.scalar.activation(out=warm[:], in_=eps_t[:], func=ACT.Abs_reciprocal_sqrt)
             if live(r - 8):
                 pass4(r - 8)

@@ -160,9 +160,10 @@ def tile_modelnew_pb_t_kernel(tc, hidden_states, kv_a_w_ckv, k_pe_raw, kv_a_ln_w
             nc.gpsimd.tensor_tensor(out=ra[:], in0=x, in1=tab[:, 1, rows, :].unsqueeze(2).to_broadcast([P, 4, 2, 32]), op=ALU.mult)
             nc.gpsimd.tensor_tensor(out=rb[:, :, 0, :], in0=x[:, :, 1, :], in1=nsin[:, rows, :], op=ALU.mult)
             nc.gpsimd.tensor_tensor(out=rb[:, :, 1, :], in0=x[:, :, 0, :], in1=tab[:, 0, rows, :], op=ALU.mult)
-            for h in range(2):
-                nc.gpsimd.tensor_tensor(out=key_sb[c][:, h, :, 128:192], in0=ra[:].rearrange("p j h i -> p j (h i)"),
-                                        in1=rb[:].rearrange("p j h i -> p j (h i)"), op=ALU.add)
+            nc.gpsimd.tensor_tensor(out=key_sb[c][:, 0, :, 128:192], in0=ra[:].rearrange("p j h i -> p j (h i)"),
+                                    in1=rb[:].rearrange("p j h i -> p j (h i)"), op=ALU.add)
+            nc.gpsimd.tensor_scalar(out=key_sb[c][:, 1, :, 128:192], in0=key_sb[c][:, 0, :, 128:192],
+                                    scalar1=1.0, scalar2=0.0, op0=ALU.mult, op1=ALU.add)
 
         def t1(k):
             xt = tpp.tile([P, 2, 2, P], F32, tag="tp")
@@ -231,7 +232,7 @@ def tile_modelnew_pb_t_kernel(tc, hidden_states, kv_a_w_ckv, k_pe_raw, kv_a_ln_w
         def pass5(k):
             c, j = divmod(k, 4)
             src = kv[k][:].rearrange("p (h e d) -> p h e d", h=2, e=2)
-            if j == 3:
+            if k % 8 == 7:
                 nc.vector.tensor_copy(out=key_sb[c][:, :, j, 0:P], in_=src[:, :, 0, :])
                 nc.vector.tensor_copy(out=v_sb[c][:, :, j, :], in_=src[:, :, 1, :])
             else:

@@ -57,10 +57,15 @@ def tile_modelnew_pb_t_kernel(tc, hidden_states, kv_a_w_ckv, k_pe_raw, kv_a_ln_w
             for e in range(2):
                 nc.sync.dma_start(out=hs_sb[2 * c + e][:].rearrange("p j d -> p (j d)"), in_=hs_v[c][:, e * 2048:(e + 1) * 2048])
 
+        def load_first_tiles():
+            for j in range(2):
+                nc.sync.dma_start(out=hs_sb[0][:, j, :], in_=hs_v[0][:, j * 1024:(j + 1) * 1024])
+            nc.sync.dma_start(out=hs_sb[1][:].rearrange("p j d -> p (j d)"), in_=hs_v[0][:, 2048:4096])
+
         wa_v = kv_a_w_ckv.rearrange("(p a) d -> a p d", a=4)
         for a in range(4):
             nc.sync.dma_start(out=wa_sb[a][:], in_=wa_v[a])
-        load_hs(0)
+        load_first_tiles()
         w_pt = const.tile([P, 4], BF16, name="w_pt")
         nc.sync.dma_start(out=w_pt[:], in_=kv_a_ln_w.rearrange("(p t) -> p t", t=4))
         nc.sync.dma_start(out=wb_sb[:], in_=kv_b_w.rearrange("(a p) k -> p a k", p=P))
@@ -153,17 +158,19 @@ def tile_modelnew_pb_t_kernel(tc, hidden_states, kv_a_w_ckv, k_pe_raw, kv_a_ln_w
             key_sb[c] = outp.tile([P, 2, 4, 192], F32, tag="key", name="key")
             v_sb[c] = outp.tile([P, 2, 4, P], F32, tag="v", name="v")
             cs = c % 4
-            x = kpe[:, c, :].rearrange("p (j h i) -> p j h i", h=2, i=32)
-            rows = slice(4 * cs, 4 * cs + 4)
-            ra = work.tile([P, 4, 2, 32], F32, tag="ra", name="ra")
-            rb = work.tile([P, 4, 2, 32], F32, tag="rb", name="rb")
-            nc.gpsimd.tensor_tensor(out=ra[:], in0=x, in1=tab[:, 1, rows, :].unsqueeze(2).to_broadcast([P, 4, 2, 32]), op=ALU.mult)
-            nc.gpsimd.tensor_tensor(out=rb[:, :, 0, :], in0=x[:, :, 1, :], in1=nsin[:, rows, :], op=ALU.mult)
-            nc.gpsimd.tensor_tensor(out=rb[:, :, 1, :], in0=x[:, :, 0, :], in1=tab[:, 0, rows, :], op=ALU.mult)
-            nc.gpsimd.tensor_tensor(out=key_sb[c][:, 0, :, 128:192], in0=ra[:].rearrange("p j h i -> p j (h i)"),
-                                    in1=rb[:].rearrange("p j h i -> p j (h i)"), op=ALU.add)
-            nc.gpsimd.tensor_scalar(out=key_sb[c][:, 1, :, 128:192], in0=key_sb[c][:, 0, :, 128:192],
-                                    scalar1=1.0, scalar2=0.0, op0=ALU.mult, op1=ALU.add)
+            for e in range(2):
+                x = kpe[:, c, e * P:(e + 1) * P].rearrange("p (j h i) -> p j h i", h=2, i=32)
+                rows = slice(4 * cs + 2 * e, 4 * cs + 2 * e + 2)
+                js = slice(2 * e, 2 * e + 2)
+                ra = work.tile([P, 2, 2, 32], F32, tag="ra", name="ra")
+                rb = work.tile([P, 2, 2, 32], F32, tag="rb", name="rb")
+                nc.gpsimd.tensor_tensor(out=ra[:], in0=x, in1=tab[:, 1, rows, :].unsqueeze(2).to_broadcast([P, 2, 2, 32]), op=ALU.mult)
+                nc.gpsimd.tensor_tensor(out=rb[:, :, 0, :], in0=x[:, :, 1, :], in1=nsin[:, rows, :], op=ALU.mult)
+                nc.gpsimd.tensor_tensor(out=rb[:, :, 1, :], in0=x[:, :, 0, :], in1=tab[:, 0, rows, :], op=ALU.mult)
+                nc.gpsimd.tensor_tensor(out=key_sb[c][:, 0, js, 128:192], in0=ra[:].rearrange("p j h i -> p j (h i)"),
+                                        in1=rb[:].rearrange("p j h i -> p j (h i)"), op=ALU.add)
+                nc.gpsimd.tensor_scalar(out=key_sb[c][:, 1, js, 128:192], in0=key_sb[c][:, 0, js, 128:192],
+                                        scalar1=1.0, scalar2=0.0, op0=ALU.mult, op1=ALU.add)
 
         def t1(k):
             xt = tpp.tile([P, 2, 2, P], F32, tag="tp")

from contextlib import ExitStack
import math

import concourse.mybir as mybir
from concourse.masks import make_identity

FLOPS = 2 * 4096 * 1024 * 512 + 2 * 4096 * 512 * 512

F32 = mybir.dt.float32
BF16 = mybir.dt.bfloat16
I32 = mybir.dt.int32
U32 = mybir.dt.uint32
U8 = mybir.dt.uint8
FP8X4 = mybir.dt.float8_e4m3fn_x4
ALU = mybir.AluOpType
ACT = mybir.ActivationFunctionType

P = 128
EPS = 1e-6
THETA = 10000.0
N_TILES = 32


def tile_modelnew_pb_t_kernel(tc, hidden_states, kv_a_w_ckv, k_pe_raw, kv_a_ln_w, kv_b_w, out_0, out_1):
    nc = tc.nc
    with ExitStack() as ctx:
        const = ctx.enter_context(tc.tile_pool(name="const", bufs=1))
        work = ctx.enter_context(tc.tile_pool(name="work", bufs=6))
        outp = ctx.enter_context(tc.tile_pool(name="outp", bufs=4))
        tpp = ctx.enter_context(tc.psum_pool(name="tpp", bufs=3))
        mxp = ctx.enter_context(tc.psum_pool(name="mxp", bufs=5))
        ctx.enter_context(tc.manual_schedule())

        s_i = const.tile([P, 16], I32, name="s_i")
        nc.gpsimd.iota(s_i[:], pattern=[[512, 4], [1, 4]], base=0, channel_multiplier=4)
        ident_f = const.tile([P, P], F32, name="ident_f")
        make_identity(nc, ident_f[:])

        one = const.tile([P, 1], F32, name="one")
        nc.vector.memset(one[:], 1.0)
        warm0 = const.tile([P, 1], F32, name="warm0")
        nc.scalar.activation(out=warm0[:], in_=one[:], func=ACT.Sin)

        hs_v = hidden_states.flatten_outer_dims().rearrange("(c p j) d -> c p (j d)", p=P, j=4)
        wa_sb = []
        for a in range(4):
            wa_a = const.tile([P, 1024], BF16, name="wa%d" % a)
            wa_sb.append(wa_a)
        wb_sb = const.tile([P, 4, 512], BF16, name="wb_sb")
        kpe = const.tile([P, 8, 256], BF16, name="kpe")
        hs_sb = []
        for h2 in range(16):
            hs_c = const.tile([P, 2, 1024], BF16, name="hs%d" % h2)
            hs_sb.append(hs_c)

        def load_hs(c):
            for e in range(2):
                nc.sync.dma_start(out=hs_sb[2 * c + e][:].rearrange("p j d -> p (j d)"), in_=hs_v[c][:, e * 2048:(e + 1) * 2048])

        def load_first_tiles():
            for j in range(2):
                nc.sync.dma_start(out=hs_sb[0][:, j, :], in_=hs_v[0][:, j * 1024:(j + 1) * 1024])
            nc.sync.dma_start(out=hs_sb[1][:].rearrange("p j d -> p (j d)"), in_=hs_v[0][:, 2048:4096])

        wa_v = kv_a_w_ckv.rearrange("(p a) d -> a p d", a=4)
        for a in range(4):
            nc.sync.dma_start(out=wa_sb[a][:], in_=wa_v[a])
        load_first_tiles()
        w_pt = const.tile([P, 4], BF16, name="w_pt")
        nc.sync.dma_start(out=w_pt[:], in_=kv_a_ln_w.rearrange("(p t) -> p t", t=4))
        nc.sync.dma_start(out=wb_sb[:], in_=kv_b_w.rearrange("(a p) k -> p a k", p=P))
        load_hs(1)
        nc.sync.dma_start(out=kpe[:], in_=k_pe_raw.flatten_outer_dims().rearrange("(c p j) r -> p c (j r)", p=P, j=4))
        for c in range(2, 8):
            load_hs(c)

        s_f = const.tile([P, 16], F32, name="s_f")
        nc.vector.tensor_copy(out=s_f[:], in_=s_i[:])
        fr = const.tile([P, 32], F32, name="fr")
        nc.vector.memset(fr[:, 0:1], 1.0)
        for m in range(5):
            n = 1 << m
            nc.vector.tensor_scalar(out=fr[:, n:2 * n], in0=fr[:, 0:n], scalar1=THETA ** (-n / 32.0), scalar2=None, op0=ALU.mult)
        nc.vector.tensor_scalar(out=fr[:], in0=fr[:], scalar1=1.0 / (2.0 * math.pi), scalar2=None, op0=ALU.mult)
        ang = const.tile([P, 2, 16, 32], F32, name="ang")
        nc.vector.tensor_tensor(out=ang[:, 0], in0=s_f[:].unsqueeze(2).to_broadcast([P, 16, 32]),
                                in1=fr[:].unsqueeze(1).to_broadcast([P, 16, 32]), op=ALU.mult)
        nc.vector.tensor_scalar(out=ang[:, 1], in0=ang[:, 0], scalar1=0.25, scalar2=None, op0=ALU.add)
        ang_f = ang[:].rearrange("p a s i -> p (a s i)")
        q_i = const.tile([P, 1024], I32, name="q_i")
        nc.vector.tensor_copy(out=q_i[:], in_=ang_f)
        k_f = const.tile([P, 1024], F32, name="k_f")
        nc.vector.tensor_copy(out=k_f[:], in_=q_i[:])
        nc.vector.tensor_tensor(out=ang_f, in0=ang_f, in1=k_f[:], op=ALU.subtract)
        eps_t = const.tile([P, 1], F32, name="eps_t")
        nc.vector.memset(eps_t[:], 1.0)
        nc.vector.tensor_scalar(out=eps_t[:], in0=eps_t[:], scalar1=EPS, scalar2=None, op0=ALU.mult)
        tab = const.tile([P, 2, 16, 32], F32, name="tab")
        nsin = const.tile([P, 16, 32], F32, name="nsin")

        def word_transposes(xt, words):
            for g in range(2):
                for u in range(2):
                    lo = 256 * g + 128 * u
                    nc.tensor.transpose(xt[:, g, u, :], words[:, lo:lo + P], ident_f[:])

        wa_grp = const.tile([P, 2, 512, 2], F32, name="wa_grp", align_bytes=64)
        wa_c = const.tile([P, 2, 512], U32, name="wa_c", align_bytes=64)
        wa_s = const.tile([P, 2, 512], U8, name="wa_s", align_bytes=64)
        for a in range(4):
            xt = tpp.tile([P, 2, 2, P], F32, tag="tp")
            word_transposes(xt, wa_sb[a][:].bitcast(F32))
            dst = wa_grp[:, :, a * P:(a + 1) * P, :]
            if a < 2:
                nc.scalar.copy(out=dst, in_=xt[:].rearrange("p g u r -> p g r u"))
            else:
                nc.vector.tensor_copy(out=dst, in_=xt[:].rearrange("p g u r -> p g r u"))
        nc.scalar.activation(out=tab[:].rearrange("p a s i -> p (a s i)"), in_=ang_f, func=ACT.Sin, scale=2.0 * math.pi)
        nc.scalar.activation(out=nsin[:], in_=ang[:, 0], func=ACT.Sin, scale=-2.0 * math.pi)
        for g in range(2):
            nc.vector.quantize_mx(out=wa_c[:, g, :].bitcast(FP8X4), scales=wa_s[:, g, :],
                                  in_=wa_grp[:, g].rearrange("p n u -> p (n u)").bitcast(BF16))

        warm = const.tile([P, 1], F32, name="warm")

        wb_grp = const.tile([P, 512, 2], F32, name="wb_grp", align_bytes=64)
        wb_c = const.tile([P, 512], U32, name="wb_c", align_bytes=64)
        wb_s = const.tile([P, 512], U8, name="wb_s", align_bytes=64)

        def prep_wb(a2):
            xt = tpp.tile([P, 2, 2, P], F32, tag="tp")
            for a in range(2):
                words = wb_sb[:, 2 * a2 + a, :].bitcast(F32).rearrange("p (w u) -> p w u", u=2)
                for u in range(2):
                    nc.tensor.transpose(xt[:, a, u, :], words[:, :, u], ident_f[:])
            nc.scalar.copy(out=wb_grp[:, a2 * 256:(a2 + 1) * 256, :].rearrange("p (a r) u -> p a r u", a=2),
                           in_=xt[:].rearrange("p a u r -> p a r u"))

        def quant_wb():
            nc.vector.quantize_mx(out=wb_c[:].bitcast(FP8X4), scales=wb_s[:],
                                  in_=wb_grp[:].rearrange("p n u -> p (n u)").bitcast(BF16))

        xtd = {}
        grp = {}
        hcode = {}
        ck = {}
        rstd = {}
        ssq = {}
        ckn = {}
        ytd = {}
        g2 = {}
        c2 = {}
        kv = {}
        key_sb = {}
        v_sb = {}

        def open_chunk(c):
            key_sb[c] = outp.tile([P, 2, 4, 192], F32, tag="key", name="key")
            v_sb[c] = outp.tile([P, 2, 4, P], F32, tag="v", name="v")
            cs = c % 4
            for e in range(2):
                x = kpe[:, c, e * P:(e + 1) * P].rearrange("p (j h i) -> p j h i", h=2, i=32)
                rows = slice(4 * cs + 2 * e, 4 * cs + 2 * e + 2)
                js = slice(2 * e, 2 * e + 2)
                ra = work.tile([P, 2, 2, 32], F32, tag="ra", name="ra")
                rb = work.tile([P, 2, 2, 32], F32, tag="rb", name="rb")
                nc.gpsimd.tensor_tensor(out=ra[:], in0=x, in1=tab[:, 1, rows, :].unsqueeze(2).to_broadcast([P, 2, 2, 32]), op=ALU.mult)
                nc.gpsimd.tensor_tensor(out=rb[:, :, 0, :], in0=x[:, :, 1, :], in1=nsin[:, rows, :], op=ALU.mult)
                nc.gpsimd.tensor_tensor(out=rb[:, :, 1, :], in0=x[:, :, 0, :], in1=tab[:, 0, rows, :], op=ALU.mult)
                nc.gpsimd.tensor_tensor(out=key_sb[c][:, 0, js, 128:192], in0=ra[:].rearrange("p j h i -> p j (h i)"),
                                        in1=rb[:].rearrange("p j h i -> p j (h i)"), op=ALU.add)
                nc.gpsimd.tensor_scalar(out=key_sb[c][:, 1, js, 128:192], in0=key_sb[c][:, 0, js, 128:192],
                                        scalar1=1.0, scalar2=0.0, op0=ALU.mult, op1=ALU.add)

        def t1(k):
            xt = tpp.tile([P, 2, 2, P], F32, tag="tp")
            word_transposes(xt, hs_sb[k // 2][:, k % 2, :].bitcast(F32))
            xtd[k] = xt

        def pass1(k):
            grp[k] = work.tile([P, 2, P, 2], F32, tag="grp", name="grp", align_bytes=64)
            if k < 2:
                nc.scalar.copy(out=grp[k][:], in_=xtd[k][:].rearrange("p g u r -> p g r u"))
            else:
                nc.vector.tensor_copy(out=grp[k][:], in_=xtd[k][:].rearrange("p g u r -> p g r u"))

        def quant_hs(k):
            hc = work.tile([P, 256], U32, tag="hc", name="hc", align_bytes=64)
            hsc = work.tile([P, 256], U8, tag="hsc", name="hsc", align_bytes=64)
            nc.vector.quantize_mx(out=hc[:].bitcast(FP8X4), scales=hsc[:],
                                  in_=grp[k][:].rearrange("p g r u -> p (g r u)").bitcast(BF16))
            hcode[k] = (hc, hsc)

        def s1(k):
            hc, hsc = hcode[k]
            acc = mxp.tile([P, 512], F32, tag="mx")
            for g in range(2):
                nc.tensor.matmul_mx(out=acc[:], lhsT=hc[:, g * P:(g + 1) * P].bitcast(FP8X4), lhsT_scale=hsc[:, g * P:(g + 1) * P],
                                    rhs=wa_c[:, g, :].bitcast(FP8X4), rhs_scale=wa_s[:, g, :], start=(g == 0), stop=(g == 1))
            ck[k] = acc

        def square(k):
            ssq[k] = work.tile([P, 1], F32, tag="ssq", name="ssq")
            junk = work.tile([P, 512], BF16, tag="junk", name="junk")
            nc.scalar.activation(out=junk[:], in_=ck[k][:], func=ACT.Square, accum_out=ssq[k][:])

        def rsqrt(k):
            rstd[k] = work.tile([P, 1], F32, tag="rs", name="rs")
            nc.scalar.activation(out=rstd[k][:], in_=ssq[k][:], func=ACT.Abs_reciprocal_sqrt, scale=1.0 / 512.0, bias=eps_t[:, 0:1])

        def pass3(k):
            ckn[k] = work.tile([P, 512], F32, tag="ckn", name="ckn")
            nc.scalar.activation(out=ckn[k][:], in_=ck[k][:], func=ACT.Copy, scale=rstd[k][:, 0:1])

        def t2(k):
            yt = tpp.tile([P, 4, P], F32, tag="tp")
            for a in range(4):
                nc.tensor.transpose(yt[:, a, :], ckn[k][:, a * P:(a + 1) * P], ident_f[:])
            ytd[k] = yt

        def pass4(k):
            g2[k] = work.tile([P, P, 4], BF16, tag="g2", name="g2", align_bytes=64)
            nc.vector.tensor_tensor(out=g2[k][:], in0=ytd[k][:].rearrange("p t r -> p r t"),
                                    in1=w_pt[:].unsqueeze(1).to_broadcast([P, P, 4]), op=ALU.mult)

        def quant2(k):
            cc = work.tile([P, P], U32, tag="cc", name="cc", align_bytes=64)
            csc = work.tile([P, P], U8, tag="csc", name="csc", align_bytes=64)
            nc.vector.quantize_mx(out=cc[:].bitcast(FP8X4), scales=csc[:], in_=g2[k][:].rearrange("p r t -> p (r t)"))
            c2[k] = (cc, csc)

        def s2(k):
            cc, csc = c2[k]
            acc = mxp.tile([P, 512], F32, tag="mx")
            nc.tensor.matmul_mx(out=acc[:], lhsT=cc[:].bitcast(FP8X4), lhsT_scale=csc[:],
                                rhs=wb_c[:].bitcast(FP8X4), rhs_scale=wb_s[:], start=True, stop=True)
            kv[k] = acc

        def pass5(k):
            c, j = divmod(k, 4)
            src = kv[k][:].rearrange("p (h e d) -> p h e d", h=2, e=2)
            if k % 8 == 7:
                nc.vector.tensor_copy(out=key_sb[c][:, :, j, 0:P], in_=src[:, :, 0, :])
                nc.vector.tensor_copy(out=v_sb[c][:, :, j, :], in_=src[:, :, 1, :])
            else:
                nc.scalar.copy(out=key_sb[c][:, :, j, 0:P], in_=src[:, :, 0, :])
                nc.scalar.copy(out=v_sb[c][:, :, j, :], in_=src[:, :, 1, :])
            b, cs = divmod(c, 4)
            rows = slice(cs * 512, (cs + 1) * 512)
            if c == 7:
                nc.sync.dma_start(out=out_0[b, :, rows, :].rearrange("h (p j) d -> j p h d", j=4)[j], in_=key_sb[c][:, :, j, :])
                nc.sync.dma_start(out=out_1[b, :, rows, :].rearrange("h (p j) d -> j p h d", j=4)[j], in_=v_sb[c][:, :, j, :])
            elif j == 3:
                nc.sync.dma_start(out=out_0[b, :, rows, :].rearrange("h (p j) d -> p h (j d)", j=4),
                                  in_=key_sb[c][:].rearrange("p h j d -> p h (j d)"))
                nc.sync.dma_start(out=out_1[b, :, rows, :].rearrange("h (p j) d -> p h (j d)", j=4),
                                  in_=v_sb[c][:].rearrange("p h j d -> p h (j d)"))

        def live(k):
            return 0 <= k < N_TILES

        for r in range(N_TILES + 14):
            if r % 4 == 0 and 0 <= r // 4 - 1 < 8:
                open_chunk(r // 4 - 1)
            if r == 7:
                quant_wb()
            if live(r - 13):
                pass5(r - 13)
            if live(r - 8):
                t2(r - 8)
            elif r == 3 or r == 4:
                prep_wb(r - 3)
            if live(r - 12):
                s2(r - 12)
            if live(r - 10):
                quant2(r - 10)
            if live(r - 4):
                s1(r - 4)
            if live(r - 3):
                quant_hs(r - 3)
            if live(r - 5):
                square(r - 5)
            if live(r - 6):
                pass3(r - 6)
            if live(r - 5):
                rsqrt(r - 5)
            if live(r):
                t1(r)
            if live(r - 1):
                pass1(r - 1)
            if r == 2:
                nc.scalar.activation(out=warm[:], in_=eps_t[:], func=ACT.Abs_reciprocal_sqrt)
            if live(r - 8):
                pass4(r - 8)
